import numpy as np
import ml_dtypes


def mxq(x, axis, fmt="e4m3"):
    dtype, down = {"e4m3": (ml_dtypes.float8_e4m3fn, 7), "e5m2": (ml_dtypes.float8_e5m2, 14)}[fmt]
    v = np.moveaxis(np.asarray(x, np.float32).astype(ml_dtypes.bfloat16).astype(np.float64), axis, -1)
    blocks = v.reshape(v.shape[:-1] + (-1, 32))
    amax = np.abs(blocks).max(-1, keepdims=True)
    byte = np.maximum(np.where(amax > 0, np.frexp(amax)[1] - 1 + 127, 0) - down, 1)
    scale = np.exp2(byte - 127.0)
    codes = (blocks / scale).astype(np.float32).astype(dtype).astype(np.float64)
    return np.moveaxis((codes * scale).reshape(v.shape), -1, axis)


WIDE = False


def mx_kscale(k):
    if not WIDE:
        return np.ones(k)
    levels = np.array([10, -10, 5, -5, 0])
    if k % 512:
        return np.exp2(np.random.permutation(np.resize(levels, k // 32))).repeat(32)
    a = np.empty((k // 512, 16))
    for p in range(k // 512):
        a[p, :8] = np.random.permutation(np.resize(levels, 8))
        for g in range(8):
            far = levels[np.abs(levels - a[p, g]) >= 10]
            a[p, g + 8] = far[np.random.randint(len(far))]
    return np.exp2(a.ravel()).repeat(32)


BF16 = ml_dtypes.bfloat16


def bf(x):
    return np.asarray(x, np.float32).astype(BF16)


def f64(x):
    return np.asarray(x).astype(np.float64)


B, T, C_IN, HIDDEN, HEADS, OUT_DIM = 4, 2048, 512, 512, 8, 512
RMS_EPS = 1.1920928955078125e-07


def silu(z):
    return z / (1.0 + np.exp(-z))


def setup_inputs():
    s, t = mx_kscale(C_IN), mx_kscale(HIDDEN)
    r = np.exp2(-12.0 * np.random.random((B, T, 1)))
    return {"x": bf(np.random.standard_normal((B, T, C_IN)) * s),
            "h_attn": bf(np.random.standard_normal((B, T, HIDDEN)) * 0.8 * r),
            "Wu": bf(np.random.standard_normal((HIDDEN, C_IN)) / np.sqrt(C_IN) / s),
            "bu": bf(np.random.standard_normal(HIDDEN) * 0.1),
            "g_norm": bf((1.0 + 0.1 * np.random.standard_normal(HIDDEN)) * t),
            "Wf": bf(np.random.standard_normal((OUT_DIM, HIDDEN)) / np.sqrt(HIDDEN) / t),
            "b_out": bf(np.random.standard_normal(OUT_DIM) * 0.1)}


def reference(x, h_attn, Wu, bu, g_norm, Wf, b_out):
    u = silu((mxq(f64(x), 2, "e4m3") @ mxq(f64(Wu), 1, "e4m3").T) + f64(bu))
    av = f64(h_attn)
    av_norm = av * (1.0 / np.sqrt(np.mean(av * av, axis=-1, keepdims=True) + RMS_EPS)) * f64(g_norm)
    uv = av_norm * u
    return (mxq(uv, 2, "e4m3") @ mxq(f64(Wf), 1, "e4m3").T) + f64(b_out)

@@ -1,0 +1,289 @@
+from contextlib import ExitStack
+
+import concourse.mybir as mybir
+from concourse.masks import make_identity
+
+FP8X4 = mybir.dt.float8_e4m3fn_x4
+BF16 = mybir.dt.bfloat16
+F32 = mybir.dt.float32
+U32 = mybir.dt.uint32
+U8 = mybir.dt.uint8
+ACT = mybir.ActivationFunctionType
+ALU = mybir.AluOpType
+
+P = 128
+PACK = 4
+WIDTH = P * PACK
+TOKENS = 4 * 2048
+TILES = 4
+GROUP = TILES * P
+N_GROUPS = TOKENS // GROUP
+N_TILES = TOKENS // P
+RMS_EPS = 1.1920928955078125e-07
+FLOPS = 2 * 2 * TOKENS * WIDTH * WIDTH
+
+
+def tile_hstu_pb_t_kernel(tc, x, h_attn, Wu, bu, g_norm, Wf, b_out, out):
+    nc = tc.nc
+    x_groups = x.flatten_outer_dims().rearrange("(n p j) c -> n p (j c)", p=P, j=TILES)
+    h_groups = h_attn.flatten_outer_dims().rearrange("(n p j) c -> n p (j c)", p=P, j=TILES)
+    out_groups = out.flatten_outer_dims().rearrange("(n p j) c -> n p (j c)", p=P, j=TILES)
+
+    with ExitStack() as ctx:
+        ctx.enter_context(tc.manual_schedule())
+        const = ctx.enter_context(tc.tile_pool(name="const", bufs=1))
+        loads = ctx.enter_context(tc.tile_pool(name="loads", bufs=5))
+        work = ctx.enter_context(tc.tile_pool(name="work", bufs=3))
+        psum = ctx.enter_context(tc.psum_pool(name="psum", bufs=2))
+
+        x_sb, h_sb, hn_sb, sumsq, rstd = {}, {}, {}, {}, {}
+        x_grouped, x_codes, x_scales = {}, {}, {}
+        u_sb, uv_grouped, uv_codes, uv_scales, o_sb = {}, {}, {}, {}, {}
+        xt_ps, z_ps, ht_ps, o_ps = {}, {}, {}, {}
+
+        def transpose_word_pair(rows, first):
+            words = rows[:].bitcast(F32)
+            bank = psum.tile([P, 2, 2, P], F32, name="xt", tag="xt", bufs=1)
+            for l in range(2):
+                for u in range(2):
+                    col = (first + l) * (WIDTH // 2)
+                    nc.tensor.transpose(bank[:, l, u, :], words[:, col + u : col + 2 * P : 2], ident[:])
+            return bank
+
+        def regroup_word_pair(copy, bank, grouped, first):
+            words = grouped[:].bitcast(F32)[:, first * 2 * P : (first + 2) * 2 * P]
+            copy(
+                out=words.rearrange("p (l w u) -> p l w u", l=2, u=2),
+                in_=bank[:].rearrange("p l u w -> p l w u"),
+            )
+
+        def transpose_f32_tile(rows, first_col):
+            bank = psum.tile([P, PACK, P], F32, name="ht", tag="ht", bufs=3)
+            for t in range(PACK):
+                col = first_col + t * P
+                nc.tensor.transpose(bank[:, t, :], rows[:, col : col + P], ident[:])
+            return bank
+
+        def load(n):
+            x_sb[n] = loads.tile([P, TILES * WIDTH], BF16, name="x_sb", tag="x_sb")
+            nc.sync.dma_start(out=x_sb[n][:], in_=x_groups[n])
+            h_sb[n] = loads.tile([P, TILES * WIDTH], BF16, name="h_sb", tag="h_sb")
+            nc.sync.dma_start(out=h_sb[n][:], in_=h_groups[n])
+
+        def square_sum(n, j):
+            if j == 0:
+                sumsq[n] = work.tile([P, TILES], F32, name="sumsq", tag="sumsq")
+            squares = work.tile([P, WIDTH], BF16, name="squares", tag="squares")
+            nc.scalar.activation(
+                out=squares[:],
+                in_=h_sb[n][:, j * WIDTH : (j + 1) * WIDTH],
+                func=ACT.Square,
+                accum_out=sumsq[n][:, j : j + 1],
+            )
+
+        def inverse_rms(n):
+            mean = work.tile([P, TILES], F32, name="mean", tag="mean")
+            nc.gpsimd.tensor_scalar(
+                out=mean[:], in0=sumsq[n][:], scalar1=1.0 / WIDTH, scalar2=RMS_EPS, op0=ALU.mult, op1=ALU.add
+            )
+            rstd[n] = work.tile([P, TILES], F32, name="rstd", tag="rstd")
+            nc.gpsimd.tensor_tensor(out=rstd[n][:], in0=mean[:], in1=minus_half[:], op=ALU.pow)
+
+        def normalise(n, j):
+            if j == 0:
+                hn_sb[n] = work.tile([P, TILES * WIDTH], F32, name="hn_sb", tag="hn_sb")
+            cols = slice(j * WIDTH, (j + 1) * WIDTH)
+            nc.gpsimd.tensor_scalar(
+                out=hn_sb[n][:, cols].rearrange("q (t p) -> q t p", t=PACK),
+                in0=h_sb[n][:, cols].rearrange("q (p t) -> q t p", t=PACK),
+                scalar1=rstd[n][:, j : j + 1],
+                scalar2=0.0,
+                op0=ALU.mult,
+                op1=ALU.add,
+            )
+
+        def transpose_x(n, first):
+            xt_ps[n, first] = transpose_word_pair(x_sb[n], first)
+
+        def regroup_x(n, first):
+            if first == 0:
+                x_grouped[n] = work.tile([P, GROUP * PACK], BF16, name="x_grouped", tag="x_grouped", align_bytes=64)
+            regroup_word_pair(nc.scalar.copy, xt_ps[n, first], x_grouped[n], first)
+
+        def quantise_x(n, first):
+            if first == 0:
+                x_codes[n] = work.tile([P, GROUP], U32, name="x_codes", tag="x_codes", align_bytes=64)
+                x_scales[n] = work.tile([P, GROUP], U8, name="x_scales", tag="x_scales", align_bytes=64)
+            toks = slice(first * P, (first + 2) * P)
+            nc.vector.quantize_mx(
+                out=x_codes[n][:, toks].bitcast(FP8X4),
+                scales=x_scales[n][:, toks],
+                in_=x_grouped[n][:, first * P * PACK : (first + 2) * P * PACK],
+            )
+
+        def project_up(n, t):
+            z_ps[n, t] = psum.tile([P, GROUP], F32, name="z", tag="z")
+            cols = slice(t * P, (t + 1) * P)
+            nc.tensor.matmul_mx(
+                out=z_ps[n, t][:],
+                lhsT=wu_codes[:, cols].bitcast(FP8X4),
+                lhsT_scale=wu_scales[:, cols],
+                rhs=x_codes[n][:].bitcast(FP8X4),
+                rhs_scale=x_scales[n][:],
+                start=True,
+                stop=True,
+            )
+
+        def silu(n, t):
+            if t == 0:
+                u_sb[n] = work.tile([P, PACK, GROUP], F32, name="u_sb", tag="u_sb")
+            nc.scalar.activation(
+                out=u_sb[n][:, t, :], in_=z_ps[n, t][:], func=ACT.Silu, bias=bias_gain[:, t : t + 1], scale=1.0
+            )
+
+        def gain(n, t):
+            nc.vector.tensor_scalar_mul(
+                out=u_sb[n][:, t, :], in0=u_sb[n][:, t, :], scalar1=bias_gain[:, PACK + t : PACK + t + 1]
+            )
+
+        def transpose_h(n, j):
+            ht_ps[n, j] = transpose_f32_tile(hn_sb[n], j * WIDTH)
+
+        def multiply(n, j):
+            if j == 0:
+                uv_grouped[n] = work.tile([P, GROUP, PACK], BF16, name="uv_grouped", tag="uv_grouped", align_bytes=64)
+            toks = slice(j * P, (j + 1) * P)
+            nc.vector.tensor_tensor(
+                out=uv_grouped[n][:, toks, :],
+                in0=u_sb[n][:, :, toks].rearrange("p t w -> p w t"),
+                in1=ht_ps[n, j][:].rearrange("p t w -> p w t"),
+                op=ALU.mult,
+            )
+
+        def quantise_uv(n, j):
+            if j == 0:
+                uv_codes[n] = work.tile([P, GROUP], U32, name="uv_codes", tag="uv_codes", align_bytes=64)
+                uv_scales[n] = work.tile([P, GROUP], U8, name="uv_scales", tag="uv_scales", align_bytes=64)
+            toks = slice(j * P, (j + 1) * P)
+            nc.vector.quantize_mx(
+                out=uv_codes[n][:, toks].bitcast(FP8X4),
+                scales=uv_scales[n][:, toks],
+                in_=uv_grouped[n][:, toks, :].rearrange("p w t -> p (w t)"),
+            )
+
+        def project_out(n, j):
+            o_ps[n, j] = psum.tile([P, WIDTH], F32, name="o", tag="o")
+            toks = slice(j * P, (j + 1) * P)
+            nc.tensor.matmul_mx(
+                out=o_ps[n, j][:],
+                lhsT=uv_codes[n][:, toks].bitcast(FP8X4),
+                lhsT_scale=uv_scales[n][:, toks],
+                rhs=wf_codes[:].bitcast(FP8X4),
+                rhs_scale=wf_scales[:],
+                start=True,
+                stop=True,
+            )
+
+        def add_bias(n, j):
+            if j == 0:
+                o_sb[n] = work.tile([P, TILES * WIDTH], F32, name="o_sb", tag="o_sb")
+            nc.vector.tensor_tensor(
+                out=o_sb[n][:, j * WIDTH : (j + 1) * WIDTH], in0=o_ps[n, j][:], in1=b_rows[:], op=ALU.add
+            )
+
+        def store(n, j):
+            cols = slice(j * WIDTH, (j + 1) * WIDTH)
+            nc.sync.dma_start(out=out_groups[n][:, cols], in_=o_sb[n][:, cols])
+
+        bu_cols = const.tile([P, PACK], BF16, name="bu_cols")
+        nc.sync.dma_start(out=bu_cols[:], in_=bu.rearrange("(p t) -> p t", t=PACK))
+        g_cols = const.tile([P, PACK], BF16, name="g_cols")
+        nc.sync.dma_start(out=g_cols[:], in_=g_norm.rearrange("(p t) -> p t", t=PACK))
+        b_row = const.tile([P, WIDTH], BF16, name="b_row")
+        nc.vector.memset(b_row[:], 0.0)
+        nc.sync.dma_start(out=b_row[0:1, :], in_=b_out.rearrange("(o c) -> o c", o=1))
+        wu_rows = const.tile([P, PACK * WIDTH], BF16, name="wu_rows")
+        nc.sync.dma_start(out=wu_rows[:], in_=Wu.rearrange("(p t) c -> p (t c)", t=PACK))
+        load(0)
+        wf_rows = const.tile([P, PACK * WIDTH], BF16, name="wf_rows")
+        nc.sync.dma_start(
+            out=wf_rows[:].rearrange("p (t c) -> p t c", t=PACK), in_=Wf.rearrange("(t p) c -> p t c", p=P)
+        )
+
+        ident = const.tile([P, P], F32, name="ident")
+        make_identity(nc, ident[:])
+        ones = const.tile([P, P], BF16, name="ones")
+        nc.vector.memset(ones[:], 1.0)
+        minus_half = const.tile([P, TILES], F32, name="minus_half")
+        nc.vector.memset(minus_half[:], -0.5)
+
+        bias_gain = const.tile([P, 2 * PACK], F32, name="bias_gain")
+        nc.vector.tensor_copy(out=bias_gain[:, 0:PACK], in_=bu_cols[:])
+        nc.vector.tensor_copy(out=bias_gain[:, PACK : 2 * PACK], in_=g_cols[:])
+
+        b_ps = psum.tile([P, WIDTH], F32, name="b_ps", tag="o")
+        nc.tensor.matmul(out=b_ps[:], lhsT=ones[:], rhs=b_row[:], start=True, stop=True)
+        b_rows = const.tile([P, WIDTH], F32, name="b_rows")
+        nc.vector.tensor_copy(out=b_rows[:], in_=b_ps[:])
+
+        wu_grouped = const.tile([P, WIDTH * PACK], BF16, name="wu_grouped", align_bytes=64)
+        wu_codes = const.tile([P, WIDTH], U32, name="wu_codes", align_bytes=64)
+        wu_scales = const.tile([P, WIDTH], U8, name="wu_scales", align_bytes=64)
+        for first in (0, 2):
+            regroup_word_pair(nc.vector.tensor_copy, transpose_word_pair(wu_rows, first), wu_grouped, first)
+        nc.vector.quantize_mx(out=wu_codes[:].bitcast(FP8X4), scales=wu_scales[:], in_=wu_grouped[:])
+
+        wf_grouped = const.tile([P, WIDTH * PACK], BF16, name="wf_grouped", align_bytes=64)
+        wf_codes = const.tile([P, WIDTH], U32, name="wf_codes", align_bytes=64)
+        wf_scales = const.tile([P, WIDTH], U8, name="wf_scales", align_bytes=64)
+
+        def regroup_wf(c):
+            words = wf_rows[:].bitcast(F32)
+            bank = psum.tile([P, 2, P], F32, name="wf_ps", tag="o")
+            for u in range(2):
+                col = c * (WIDTH // 2)
+                nc.tensor.transpose(bank[:, u, :], words[:, col + u : col + 2 * P : 2], ident[:])
+            grouped = wf_grouped[:].bitcast(F32)[:, c * 2 * P : (c + 1) * 2 * P]
+            nc.vector.tensor_copy(out=grouped.rearrange("p (w u) -> p w u", u=2), in_=bank[:].rearrange("p u w -> p w u"))
+
+        def quantise_wf():
+            nc.vector.quantize_mx(
+                out=wf_codes[:].bitcast(FP8X4), scales=wf_scales[:], in_=wf_grouped[:]
+            )
+
+        def at(stage, tile_index):
+            n, j = divmod(tile_index, TILES)
+            if 0 <= n < N_GROUPS:
+                stage(n, j)
+
+        def at_pair(stage, tile_index):
+            if tile_index % 2 == 0:
+                at(stage, tile_index)
+
+        def at_group(stage, tile_index):
+            n, j = divmod(tile_index, TILES)
+            if j == 0 and 0 <= n < N_GROUPS:
+                stage(n)
+
+        for s in range(-3 * TILES, N_TILES + 3):
+            if s + 4 * TILES > 0:
+                at_group(load, s + 4 * TILES)
+            at(transpose_h, s + 2)
+            at_pair(transpose_x, s + 11)
+            at(project_up, s + 6)
+            at(project_out, s - 2)
+            at(square_sum, s + 7)
+            at_pair(regroup_x, s + 10)
+            at(silu, s + 5)
+            at_group(inverse_rms, s + 3)
+            at(normalise, s + 3)
+            at(multiply, s)
+            at(add_bias, s - 3)
+            at(gain, s + 4)
+            at(quantise_uv, s - 1)
+            at_pair(quantise_x, s + 9)
+            at(store, s - 3)
+            if -TILES <= s < 0:
+                regroup_wf(s + TILES)
+            if s == -1:
+                quantise_wf()

@@ -19,6 +19,7 @@ TILES = 4
 GROUP = TILES * P
 N_GROUPS = TOKENS // GROUP
 N_TILES = TOKENS // P
+LINE = 4
 RMS_EPS = 1.1920928955078125e-07
 FLOPS = 2 * 2 * TOKENS * WIDTH * WIDTH
 
@@ -94,8 +95,8 @@ def tile_hstu_pb_t_kernel(tc, x, h_attn, Wu, bu, g_norm, Wf, b_out, out):
                 hn_sb[n] = work.tile([P, TILES * WIDTH], F32, name="hn_sb", tag="hn_sb")
             cols = slice(j * WIDTH, (j + 1) * WIDTH)
             nc.gpsimd.tensor_scalar(
-                out=hn_sb[n][:, cols].rearrange("q (t p) -> q t p", t=PACK),
-                in0=h_sb[n][:, cols].rearrange("q (p t) -> q t p", t=PACK),
+                out=hn_sb[n][:, cols].rearrange("q (t c i) -> q c t i", t=PACK, i=LINE),
+                in0=h_sb[n][:, cols].rearrange("q (c i t) -> q c t i", t=PACK, i=LINE),
                 scalar1=rstd[n][:, j : j + 1],
                 scalar2=0.0,
                 op0=ALU.mult,
@@ -154,9 +155,9 @@ def tile_hstu_pb_t_kernel(tc, x, h_attn, Wu, bu, g_norm, Wf, b_out, out):
                 uv_grouped[n] = work.tile([P, GROUP, PACK], BF16, name="uv_grouped", tag="uv_grouped", align_bytes=64)
             toks = slice(j * P, (j + 1) * P)
             nc.vector.tensor_tensor(
-                out=uv_grouped[n][:, toks, :],
-                in0=u_sb[n][:, :, toks].rearrange("p t w -> p w t"),
-                in1=ht_ps[n, j][:].rearrange("p t w -> p w t"),
+                out=uv_grouped[n][:, toks, :].rearrange("p (c i) t -> p c t i", i=LINE),
+                in0=u_sb[n][:, :, toks].rearrange("p t (c i) -> p c t i", i=LINE),
+                in1=ht_ps[n, j][:].rearrange("p t (c i) -> p c t i", i=LINE),
                 op=ALU.mult,
             )
 

@@ -15,25 +15,26 @@ P = 128
 PACK = 4
 WIDTH = P * PACK
 TOKENS = 4 * 2048
-TILES = 4
-GROUP = TILES * P
-N_GROUPS = TOKENS // GROUP
-N_TILES = TOKENS // P
+LOAD_TILES = 4
+N_LOADS = TOKENS // (LOAD_TILES * P)
+PAIR = 2 * P
+N_PAIRS = TOKENS // PAIR
 LINE = 4
+AHEAD = 4
 RMS_EPS = 1.1920928955078125e-07
 FLOPS = 2 * 2 * TOKENS * WIDTH * WIDTH
 
 
 def tile_hstu_pb_t_kernel(tc, x, h_attn, Wu, bu, g_norm, Wf, b_out, out):
     nc = tc.nc
-    x_groups = x.flatten_outer_dims().rearrange("(n p j) c -> n p (j c)", p=P, j=TILES)
-    h_groups = h_attn.flatten_outer_dims().rearrange("(n p j) c -> n p (j c)", p=P, j=TILES)
-    out_groups = out.flatten_outer_dims().rearrange("(n p j) c -> n p (j c)", p=P, j=TILES)
+    x_loads = x.flatten_outer_dims().rearrange("(n p j) c -> n p (j c)", p=P, j=LOAD_TILES)
+    h_loads = h_attn.flatten_outer_dims().rearrange("(n p j) c -> n p (j c)", p=P, j=LOAD_TILES)
+    out_loads = out.flatten_outer_dims().rearrange("(n p j) c -> n p (j c)", p=P, j=LOAD_TILES)
 
     with ExitStack() as ctx:
         ctx.enter_context(tc.manual_schedule())
         const = ctx.enter_context(tc.tile_pool(name="const", bufs=1))
-        loads = ctx.enter_context(tc.tile_pool(name="loads", bufs=5))
+        loads = ctx.enter_context(tc.tile_pool(name="loads", bufs=6))
         work = ctx.enter_context(tc.tile_pool(name="work", bufs=3))
         psum = ctx.enter_context(tc.psum_pool(name="psum", bufs=2))
 
@@ -42,249 +43,250 @@ def tile_hstu_pb_t_kernel(tc, x, h_attn, Wu, bu, g_norm, Wf, b_out, out):
         u_sb, uv_grouped, uv_codes, uv_scales, o_sb = {}, {}, {}, {}, {}
         xt_ps, z_ps, ht_ps, o_ps = {}, {}, {}, {}
 
-        def transpose_word_pair(rows, first):
+        def transpose_word_pair(bank, rows, first_col):
             words = rows[:].bitcast(F32)
-            bank = psum.tile([P, 2, 2, P], F32, name="xt", tag="xt", bufs=1)
             for l in range(2):
-                for u in range(2):
-                    col = (first + l) * (WIDTH // 2)
-                    nc.tensor.transpose(bank[:, l, u, :], words[:, col + u : col + 2 * P : 2], ident[:])
-            return bank
+                for v in range(2):
+                    col = first_col // 2 + l * (WIDTH // 2)
+                    nc.tensor.transpose(bank[:, l, v, :], words[:, col + v : col + 2 * P : 2], ident[:])
 
         def regroup_word_pair(copy, bank, grouped, first):
             words = grouped[:].bitcast(F32)[:, first * 2 * P : (first + 2) * 2 * P]
             copy(
-                out=words.rearrange("p (l w u) -> p l w u", l=2, u=2),
-                in_=bank[:].rearrange("p l u w -> p l w u"),
+                out=words.rearrange("p (l w v) -> p l w v", l=2, v=2),
+                in_=bank[:].rearrange("p l v w -> p l w v"),
             )
-
-        def transpose_f32_tile(rows, first_col):
-            bank = psum.tile([P, PACK, P], F32, name="ht", tag="ht", bufs=3)
-            for t in range(PACK):
-                col = first_col + t * P
-                nc.tensor.transpose(bank[:, t, :], rows[:, col : col + P], ident[:])
-            return bank
 
         def load(n):
-            x_sb[n] = loads.tile([P, TILES * WIDTH], BF16, name="x_sb", tag="x_sb")
-            nc.sync.dma_start(out=x_sb[n][:], in_=x_groups[n])
-            h_sb[n] = loads.tile([P, TILES * WIDTH], BF16, name="h_sb", tag="h_sb")
-            nc.sync.dma_start(out=h_sb[n][:], in_=h_groups[n])
+            x_sb[n] = loads.tile([P, LOAD_TILES * WIDTH], BF16, name="x_sb", tag="x_sb")
+            h_sb[n] = loads.tile([P, LOAD_TILES * WIDTH], BF16, name="h_sb", tag="h_sb")
+            nc.sync.dma_start(out=x_sb[n][:], in_=x_loads[n])
+            nc.sync.dma_start(out=h_sb[n][:], in_=h_loads[n])
 
-        def square_sum(n, j):
+        def tile_cols(q, j):
+            first = (2 * (q % 2) + j) * WIDTH
+            return slice(first, first + WIDTH)
+
+        def square_sum(q, j):
             if j == 0:
-                sumsq[n] = work.tile([P, TILES], F32, name="sumsq", tag="sumsq")
+                sumsq[q] = work.tile([P, 2], F32, name="sumsq", tag="sumsq")
             squares = work.tile([P, WIDTH], BF16, name="squares", tag="squares")
             nc.scalar.activation(
-                out=squares[:],
-                in_=h_sb[n][:, j * WIDTH : (j + 1) * WIDTH],
-                func=ACT.Square,
-                accum_out=sumsq[n][:, j : j + 1],
+                out=squares[:], in_=h_sb[q // 2][:, tile_cols(q, j)], func=ACT.Square, accum_out=sumsq[q][:, j : j + 1]
             )
 
-        def inverse_rms(n):
-            mean = work.tile([P, TILES], F32, name="mean", tag="mean")
+        def inverse_rms(q):
+            mean = work.tile([P, 2], F32, name="mean", tag="mean")
             nc.gpsimd.tensor_scalar(
-                out=mean[:], in0=sumsq[n][:], scalar1=1.0 / WIDTH, scalar2=RMS_EPS, op0=ALU.mult, op1=ALU.add
+                out=mean[:], in0=sumsq[q][:], scalar1=1.0 / WIDTH, scalar2=RMS_EPS, op0=ALU.mult, op1=ALU.add
             )
-            rstd[n] = work.tile([P, TILES], F32, name="rstd", tag="rstd")
-            nc.gpsimd.tensor_tensor(out=rstd[n][:], in0=mean[:], in1=minus_half[:], op=ALU.pow)
+            rstd[q] = work.tile([P, 2], F32, name="rstd", tag="rstd")
+            nc.gpsimd.tensor_tensor(out=rstd[q][:], in0=mean[:], in1=minus_half[:], op=ALU.pow)
 
-        def normalise(n, j):
+        def normalise(q, j):
             if j == 0:
-                hn_sb[n] = work.tile([P, TILES * WIDTH], F32, name="hn_sb", tag="hn_sb")
-            cols = slice(j * WIDTH, (j + 1) * WIDTH)
+                hn_sb[q] = work.tile([P, 2, WIDTH], F32, name="hn_sb", tag="hn_sb")
             nc.gpsimd.tensor_scalar(
-                out=hn_sb[n][:, cols].rearrange("q (t c i) -> q c t i", t=PACK, i=LINE),
-                in0=h_sb[n][:, cols].rearrange("q (c i t) -> q c t i", t=PACK, i=LINE),
-                scalar1=rstd[n][:, j : j + 1],
+                out=hn_sb[q][:, j, :].rearrange("r (t c i) -> r c t i", t=PACK, i=LINE),
+                in0=h_sb[q // 2][:, tile_cols(q, j)].rearrange("r (c i t) -> r c t i", t=PACK, i=LINE),
+                scalar1=rstd[q][:, j : j + 1],
                 scalar2=0.0,
                 op0=ALU.mult,
                 op1=ALU.add,
             )
 
-        def transpose_x(n, first):
-            xt_ps[n, first] = transpose_word_pair(x_sb[n], first)
+        def transpose_x(q):
+            xt_ps[q] = psum.tile([P, 2, 2, P], F32, name="xt", tag="xt", bufs=1)
+            transpose_word_pair(xt_ps[q], x_sb[q // 2], tile_cols(q, 0).start)
 
-        def regroup_x(n, first):
-            if first == 0:
-                x_grouped[n] = work.tile([P, GROUP * PACK], BF16, name="x_grouped", tag="x_grouped", align_bytes=64)
-            regroup_word_pair(nc.scalar.copy, xt_ps[n, first], x_grouped[n], first)
+        def regroup_x(q):
+            x_grouped[q] = work.tile([P, PAIR * PACK], BF16, name="x_grouped", tag="x_grouped", align_bytes=64)
+            regroup_word_pair(nc.scalar.copy, xt_ps[q], x_grouped[q], 0)
 
-        def quantise_x(n, first):
-            if first == 0:
-                x_codes[n] = work.tile([P, GROUP], U32, name="x_codes", tag="x_codes", align_bytes=64)
-                x_scales[n] = work.tile([P, GROUP], U8, name="x_scales", tag="x_scales", align_bytes=64)
-            toks = slice(first * P, (first + 2) * P)
-            nc.vector.quantize_mx(
-                out=x_codes[n][:, toks].bitcast(FP8X4),
-                scales=x_scales[n][:, toks],
-                in_=x_grouped[n][:, first * P * PACK : (first + 2) * P * PACK],
-            )
+        def quantise_x(q):
+            x_codes[q] = work.tile([P, PAIR], U32, name="x_codes", tag="x_codes", align_bytes=64)
+            x_scales[q] = work.tile([P, PAIR], U8, name="x_scales", tag="x_scales", align_bytes=64)
+            nc.vector.quantize_mx(out=x_codes[q][:].bitcast(FP8X4), scales=x_scales[q][:], in_=x_grouped[q][:])
 
-        def project_up(n, t):
-            z_ps[n, t] = psum.tile([P, GROUP], F32, name="z", tag="z")
+        def project_up(q, t):
+            if t % 2 == 0:
+                z_ps[q, t // 2] = psum.tile([P, 2, PAIR], F32, name="z", tag="z")
             cols = slice(t * P, (t + 1) * P)
             nc.tensor.matmul_mx(
-                out=z_ps[n, t][:],
+                out=z_ps[q, t // 2][:, t % 2, :],
                 lhsT=wu_codes[:, cols].bitcast(FP8X4),
                 lhsT_scale=wu_scales[:, cols],
-                rhs=x_codes[n][:].bitcast(FP8X4),
-                rhs_scale=x_scales[n][:],
+                rhs=x_codes[q][:].bitcast(FP8X4),
+                rhs_scale=x_scales[q][:],
                 start=True,
                 stop=True,
             )
 
-        def silu(n, t):
+        def silu(q, t):
             if t == 0:
-                u_sb[n] = work.tile([P, PACK, GROUP], F32, name="u_sb", tag="u_sb")
+                u_sb[q] = work.tile([P, PACK, PAIR], F32, name="u_sb", tag="u_sb")
             nc.scalar.activation(
-                out=u_sb[n][:, t, :], in_=z_ps[n, t][:], func=ACT.Silu, bias=bias_gain[:, t : t + 1], scale=1.0
+                out=u_sb[q][:, t, :], in_=z_ps[q, t // 2][:, t % 2, :], func=ACT.Silu, bias=bu_cols[:, t : t + 1], scale=1.0
             )
 
-        def gain(n, t):
-            nc.vector.tensor_scalar_mul(
-                out=u_sb[n][:, t, :], in0=u_sb[n][:, t, :], scalar1=bias_gain[:, PACK + t : PACK + t + 1]
-            )
+        def gain(q, t):
+            nc.vector.tensor_scalar_mul(out=u_sb[q][:, t, :], in0=u_sb[q][:, t, :], scalar1=g_cols[:, t : t + 1])
 
-        def transpose_h(n, j):
-            ht_ps[n, j] = transpose_f32_tile(hn_sb[n], j * WIDTH)
+        def transpose_h(q, j):
+            ht_ps[q, j] = psum.tile([P, PACK, P], F32, name="ht", tag="ht", bufs=3)
+            for t in range(PACK):
+                nc.tensor.transpose(ht_ps[q, j][:, t, :], hn_sb[q][:, j, t * P : (t + 1) * P], ident[:])
 
-        def multiply(n, j):
+        def multiply(q, j):
             if j == 0:
-                uv_grouped[n] = work.tile([P, GROUP, PACK], BF16, name="uv_grouped", tag="uv_grouped", align_bytes=64)
+                uv_grouped[q] = work.tile([P, PAIR, PACK], BF16, name="uv_grouped", tag="uv_grouped", align_bytes=64)
             toks = slice(j * P, (j + 1) * P)
             nc.vector.tensor_tensor(
-                out=uv_grouped[n][:, toks, :].rearrange("p (c i) t -> p c t i", i=LINE),
-                in0=u_sb[n][:, :, toks].rearrange("p t (c i) -> p c t i", i=LINE),
-                in1=ht_ps[n, j][:].rearrange("p t (c i) -> p c t i", i=LINE),
+                out=uv_grouped[q][:, toks, :].rearrange("p (c i) t -> p c t i", i=LINE),
+                in0=u_sb[q][:, :, toks].rearrange("p t (c i) -> p c t i", i=LINE),
+                in1=ht_ps[q, j][:].rearrange("p t (c i) -> p c t i", i=LINE),
                 op=ALU.mult,
             )
 
-        def quantise_uv(n, j):
-            if j == 0:
-                uv_codes[n] = work.tile([P, GROUP], U32, name="uv_codes", tag="uv_codes", align_bytes=64)
-                uv_scales[n] = work.tile([P, GROUP], U8, name="uv_scales", tag="uv_scales", align_bytes=64)
-            toks = slice(j * P, (j + 1) * P)
+        def quantise_uv(q):
+            uv_codes[q] = work.tile([P, PAIR], U32, name="uv_codes", tag="uv_codes", align_bytes=64)
+            uv_scales[q] = work.tile([P, PAIR], U8, name="uv_scales", tag="uv_scales", align_bytes=64)
             nc.vector.quantize_mx(
-                out=uv_codes[n][:, toks].bitcast(FP8X4),
-                scales=uv_scales[n][:, toks],
-                in_=uv_grouped[n][:, toks, :].rearrange("p w t -> p (w t)"),
+                out=uv_codes[q][:].bitcast(FP8X4),
+                scales=uv_scales[q][:],
+                in_=uv_grouped[q][:].rearrange("p w t -> p (w t)"),
             )
 
-        def project_out(n, j):
-            o_ps[n, j] = psum.tile([P, WIDTH], F32, name="o", tag="o")
+        def project_out(q, j):
+            o_ps[q, j] = psum.tile([P, WIDTH], F32, name="o", tag="o")
             toks = slice(j * P, (j + 1) * P)
             nc.tensor.matmul_mx(
-                out=o_ps[n, j][:],
-                lhsT=uv_codes[n][:, toks].bitcast(FP8X4),
-                lhsT_scale=uv_scales[n][:, toks],
+                out=o_ps[q, j][:],
+                lhsT=uv_codes[q][:, toks].bitcast(FP8X4),
+                lhsT_scale=uv_scales[q][:, toks],
                 rhs=wf_codes[:].bitcast(FP8X4),
                 rhs_scale=wf_scales[:],
                 start=True,
                 stop=True,
             )
 
-        def add_bias(n, j):
+        def add_bias(q, j):
             if j == 0:
-                o_sb[n] = work.tile([P, TILES * WIDTH], F32, name="o_sb", tag="o_sb")
-            nc.vector.tensor_tensor(
-                out=o_sb[n][:, j * WIDTH : (j + 1) * WIDTH], in0=o_ps[n, j][:], in1=b_rows[:], op=ALU.add
+                o_sb[q] = work.tile([P, 2, WIDTH], F32, name="o_sb", tag="o_sb")
+            nc.vector.tensor_tensor(out=o_sb[q][:, j, :], in0=o_ps[q, j][:], in1=b_rows[:], op=ALU.add)
+
+        def store(q):
+            first = 2 * (q % 2) * WIDTH
+            nc.sync.dma_start(
+                out=out_loads[q // 2][:, first : first + 2 * WIDTH], in_=o_sb[q][:].rearrange("p j c -> p (j c)")
             )
 
-        def store(n, j):
-            cols = slice(j * WIDTH, (j + 1) * WIDTH)
-            nc.sync.dma_start(out=out_groups[n][:, cols], in_=o_sb[n][:, cols])
-
+        x_sb[0] = loads.tile([P, LOAD_TILES * WIDTH], BF16, name="x_sb", tag="x_sb")
+        h_sb[0] = loads.tile([P, LOAD_TILES * WIDTH], BF16, name="h_sb", tag="h_sb")
+        wu_rows = const.tile([P, PACK * WIDTH], BF16, name="wu_rows")
+        wf_rows = const.tile([P, PACK * WIDTH], BF16, name="wf_rows")
         bu_cols = const.tile([P, PACK], BF16, name="bu_cols")
-        nc.sync.dma_start(out=bu_cols[:], in_=bu.rearrange("(p t) -> p t", t=PACK))
         g_cols = const.tile([P, PACK], BF16, name="g_cols")
-        nc.sync.dma_start(out=g_cols[:], in_=g_norm.rearrange("(p t) -> p t", t=PACK))
         b_row = const.tile([P, WIDTH], BF16, name="b_row")
         nc.vector.memset(b_row[:], 0.0)
-        nc.sync.dma_start(out=b_row[0:1, :], in_=b_out.rearrange("(o c) -> o c", o=1))
-        wu_rows = const.tile([P, PACK * WIDTH], BF16, name="wu_rows")
+        first_pair, second_pair = slice(0, 2 * WIDTH), slice(2 * WIDTH, 4 * WIDTH)
+        nc.sync.dma_start(out=h_sb[0][:, first_pair], in_=h_loads[0][:, first_pair])
         nc.sync.dma_start(out=wu_rows[:], in_=Wu.rearrange("(p t) c -> p (t c)", t=PACK))
-        load(0)
-        wf_rows = const.tile([P, PACK * WIDTH], BF16, name="wf_rows")
+        nc.sync.dma_start(out=x_sb[0][:, first_pair], in_=x_loads[0][:, first_pair])
+        nc.sync.dma_start(out=bu_cols[:], in_=bu.rearrange("(p t) -> p t", t=PACK))
+        nc.sync.dma_start(out=g_cols[:], in_=g_norm.rearrange("(p t) -> p t", t=PACK))
+        nc.sync.dma_start(out=b_row[0:1, :], in_=b_out.rearrange("(o c) -> o c", o=1))
+        nc.sync.dma_start(out=x_sb[0][:, second_pair], in_=x_loads[0][:, second_pair])
         nc.sync.dma_start(
             out=wf_rows[:].rearrange("p (t c) -> p t c", t=PACK), in_=Wf.rearrange("(t p) c -> p t c", p=P)
         )
+        nc.sync.dma_start(out=h_sb[0][:, second_pair], in_=h_loads[0][:, second_pair])
+        for n in range(1, AHEAD):
+            load(n)
 
         ident = const.tile([P, P], F32, name="ident")
         make_identity(nc, ident[:])
         ones = const.tile([P, P], BF16, name="ones")
         nc.vector.memset(ones[:], 1.0)
-        minus_half = const.tile([P, TILES], F32, name="minus_half")
+        minus_half = const.tile([P, 2], F32, name="minus_half")
         nc.vector.memset(minus_half[:], -0.5)
-
-        bias_gain = const.tile([P, 2 * PACK], F32, name="bias_gain")
-        nc.vector.tensor_copy(out=bias_gain[:, 0:PACK], in_=bu_cols[:])
-        nc.vector.tensor_copy(out=bias_gain[:, PACK : 2 * PACK], in_=g_cols[:])
-
-        b_ps = psum.tile([P, WIDTH], F32, name="b_ps", tag="o")
-        nc.tensor.matmul(out=b_ps[:], lhsT=ones[:], rhs=b_row[:], start=True, stop=True)
-        b_rows = const.tile([P, WIDTH], F32, name="b_rows")
-        nc.vector.tensor_copy(out=b_rows[:], in_=b_ps[:])
+        table = const.tile([P, 1], F32, name="table")
+        nc.scalar.activation(out=table[:], in_=minus_half[:, 0:1], func=ACT.Silu)
 
         wu_grouped = const.tile([P, WIDTH * PACK], BF16, name="wu_grouped", align_bytes=64)
         wu_codes = const.tile([P, WIDTH], U32, name="wu_codes", align_bytes=64)
         wu_scales = const.tile([P, WIDTH], U8, name="wu_scales", align_bytes=64)
-        for first in (0, 2):
-            regroup_word_pair(nc.vector.tensor_copy, transpose_word_pair(wu_rows, first), wu_grouped, first)
-        nc.vector.quantize_mx(out=wu_codes[:].bitcast(FP8X4), scales=wu_scales[:], in_=wu_grouped[:])
-
         wf_grouped = const.tile([P, WIDTH * PACK], BF16, name="wf_grouped", align_bytes=64)
         wf_codes = const.tile([P, WIDTH], U32, name="wf_codes", align_bytes=64)
         wf_scales = const.tile([P, WIDTH], U8, name="wf_scales", align_bytes=64)
+        b_rows = const.tile([P, WIDTH], F32, name="b_rows")
 
-        def regroup_wf(c):
-            words = wf_rows[:].bitcast(F32)
-            bank = psum.tile([P, 2, P], F32, name="wf_ps", tag="o")
-            for u in range(2):
-                col = c * (WIDTH // 2)
-                nc.tensor.transpose(bank[:, u, :], words[:, col + u : col + 2 * P : 2], ident[:])
-            grouped = wf_grouped[:].bitcast(F32)[:, c * 2 * P : (c + 1) * 2 * P]
-            nc.vector.tensor_copy(out=grouped.rearrange("p (w u) -> p w u", u=2), in_=bank[:].rearrange("p u w -> p w u"))
+        square_sum(0, 0)
+        square_sum(0, 1)
+        wu_banks, wf_banks = {}, {}
+        for half in range(2):
+            wu_banks[half] = psum.tile([P, 2, 2, P], F32, name="wu_ps", tag="z")
+            transpose_word_pair(wu_banks[half], wu_rows, 2 * half * WIDTH)
+        regroup_word_pair(nc.vector.tensor_copy, wu_banks[0], wu_grouped, 0)
+        regroup_word_pair(nc.scalar.copy, wu_banks[1], wu_grouped, 2)
+        nc.vector.quantize_mx(out=wu_codes[:].bitcast(FP8X4), scales=wu_scales[:], in_=wu_grouped[:])
+        inverse_rms(0)
+        for j in range(2):
+            normalise(0, j)
+        for q in range(2):
+            transpose_x(q)
+            regroup_x(q)
+        quantise_x(0)
+        for t in range(PACK):
+            project_up(0, t)
+        for t in range(PACK):
+            silu(0, t)
 
-        def quantise_wf():
-            nc.vector.quantize_mx(
-                out=wf_codes[:].bitcast(FP8X4), scales=wf_scales[:], in_=wf_grouped[:]
-            )
+        for half in range(2):
+            wf_banks[half] = psum.tile([P, 2, 2, P], F32, name="wf_ps", tag="o")
+            transpose_word_pair(wf_banks[half], wf_rows, 2 * half * WIDTH)
+            regroup_word_pair(nc.vector.tensor_copy, wf_banks[half], wf_grouped, 2 * half)
+        b_ps = psum.tile([P, WIDTH], F32, name="b_ps", tag="ht", bufs=3)
+        nc.tensor.matmul(out=b_ps[:], lhsT=ones[:], rhs=b_row[:], start=True, stop=True)
+        nc.vector.quantize_mx(out=wf_codes[:].bitcast(FP8X4), scales=wf_scales[:], in_=wf_grouped[:])
+        nc.vector.tensor_copy(out=b_rows[:], in_=b_ps[:])
+        for j in range(2):
+            transpose_h(0, j)
+        for t in range(PACK):
+            gain(0, t)
+        for q in (1, 2):
+            for j in range(2):
+                square_sum(q, j)
+        inverse_rms(1)
 
-        def at(stage, tile_index):
-            n, j = divmod(tile_index, TILES)
-            if 0 <= n < N_GROUPS:
-                stage(n, j)
+        def at(stage, q, *args):
+            if 0 <= q < N_PAIRS:
+                stage(q, *args)
 
-        def at_pair(stage, tile_index):
-            if tile_index % 2 == 0:
-                at(stage, tile_index)
-
-        def at_group(stage, tile_index):
-            n, j = divmod(tile_index, TILES)
-            if j == 0 and 0 <= n < N_GROUPS:
-                stage(n)
-
-        for s in range(-3 * TILES, N_TILES + 3):
-            if s + 4 * TILES > 0:
-                at_group(load, s + 4 * TILES)
-            at(transpose_h, s + 2)
-            at_pair(transpose_x, s + 11)
-            at(project_up, s + 6)
-            at(project_out, s - 2)
-            at(square_sum, s + 7)
-            at_pair(regroup_x, s + 10)
-            at(silu, s + 5)
-            at_group(inverse_rms, s + 3)
-            at(normalise, s + 3)
-            at(multiply, s)
-            at(add_bias, s - 3)
-            at(gain, s + 4)
-            at(quantise_uv, s - 1)
-            at_pair(quantise_x, s + 9)
-            at(store, s - 3)
-            if -TILES <= s < 0:
-                regroup_wf(s + TILES)
-            if s == -1:
-                quantise_wf()
+        for p in range(N_PAIRS + 1):
+            if p % 2 == 0 and p // 2 + AHEAD < N_LOADS:
+                load(p // 2 + AHEAD)
+            at(quantise_x, p + 1)
+            for j in range(2):
+                at(multiply, p, j)
+            for j in range(2):
+                at(project_out, p - 1, j)
+            for t in range(PACK):
+                at(project_up, p + 1, t)
+            at(transpose_x, p + 2)
+            for j in range(2):
+                at(normalise, p + 1, j)
+            for j in range(2):
+                at(transpose_h, p + 1, j)
+            at(inverse_rms, p + 2)
+            at(square_sum, p + 3, 0)
+            for t in range(PACK):
+                at(silu, p + 1, t)
+            at(regroup_x, p + 2)
+            at(square_sum, p + 3, 1)
+            for j in range(2):
+                at(add_bias, p - 1, j)
+            at(quantise_uv, p)
+            for t in range(PACK):
+                at(gain, p + 1, t)
+            at(store, p - 1)

@@ -20,7 +20,9 @@ N_LOADS = TOKENS // (LOAD_TILES * P)
 PAIR = 2 * P
 N_PAIRS = TOKENS // PAIR
 LINE = 4
-AHEAD = 4
+AHEAD = 5
+MAX_BATCH = 4
+BATCHES = (1, 2, 2, 3) + (MAX_BATCH,) * 6
 RMS_EPS = 1.1920928955078125e-07
 FLOPS = 2 * 2 * TOKENS * WIDTH * WIDTH
 
@@ -34,12 +36,14 @@ def tile_hstu_pb_t_kernel(tc, x, h_attn, Wu, bu, g_norm, Wf, b_out, out):
     with ExitStack() as ctx:
         ctx.enter_context(tc.manual_schedule())
         const = ctx.enter_context(tc.tile_pool(name="const", bufs=1))
-        loads = ctx.enter_context(tc.tile_pool(name="loads", bufs=6))
+        loads = ctx.enter_context(tc.tile_pool(name="loads", bufs=7))
         work = ctx.enter_context(tc.tile_pool(name="work", bufs=3))
         psum = ctx.enter_context(tc.psum_pool(name="psum", bufs=2))
 
         x_sb, h_sb, hn_sb, sumsq, rstd = {}, {}, {}, {}, {}
         x_grouped, x_codes, x_scales = {}, {}, {}
+        first_of = [sum(BATCHES[:b]) for b in range(len(BATCHES))]
+        batch_of = [b for b in range(len(BATCHES)) for q in range(BATCHES[b])]
         u_sb, uv_grouped, uv_codes, uv_scales, o_sb = {}, {}, {}, {}, {}
         xt_ps, z_ps, ht_ps, o_ps = {}, {}, {}, {}
 
@@ -67,29 +71,35 @@ def tile_hstu_pb_t_kernel(tc, x, h_attn, Wu, bu, g_norm, Wf, b_out, out):
             first = (2 * (q % 2) + j) * WIDTH
             return slice(first, first + WIDTH)
 
-        def square_sum(q, j):
-            if j == 0:
-                sumsq[q] = work.tile([P, 2], F32, name="sumsq", tag="sumsq")
+        def square_sum(tile):
+            q, j = divmod(tile, 2)
+            b = batch_of[q]
+            if b not in sumsq:
+                sumsq[b] = work.tile([P, 2 * MAX_BATCH], F32, name="sumsq", tag="sumsq")
+            col = tile - 2 * first_of[b]
             squares = work.tile([P, WIDTH], BF16, name="squares", tag="squares")
             nc.scalar.activation(
-                out=squares[:], in_=h_sb[q // 2][:, tile_cols(q, j)], func=ACT.Square, accum_out=sumsq[q][:, j : j + 1]
+                out=squares[:], in_=h_sb[q // 2][:, tile_cols(q, j)], func=ACT.Square, accum_out=sumsq[b][:, col : col + 1]
             )
 
-        def inverse_rms(q):
-            mean = work.tile([P, 2], F32, name="mean", tag="mean")
+        def inverse_rms(b):
+            n = 2 * BATCHES[b]
+            mean = work.tile([P, 2 * MAX_BATCH], F32, name="mean", tag="mean")
             nc.gpsimd.tensor_scalar(
-                out=mean[:], in0=sumsq[q][:], scalar1=1.0 / WIDTH, scalar2=RMS_EPS, op0=ALU.mult, op1=ALU.add
+                out=mean[:, 0:n], in0=sumsq[b][:, 0:n], scalar1=1.0 / WIDTH, scalar2=RMS_EPS, op0=ALU.mult, op1=ALU.add
             )
-            rstd[q] = work.tile([P, 2], F32, name="rstd", tag="rstd")
-            nc.gpsimd.tensor_tensor(out=rstd[q][:], in0=mean[:], in1=minus_half[:], op=ALU.pow)
+            rstd[b] = work.tile([P, 2 * MAX_BATCH], F32, name="rstd", tag="rstd")
+            nc.gpsimd.tensor_tensor(out=rstd[b][:, 0:n], in0=mean[:, 0:n], in1=minus_half[:, 0:n], op=ALU.pow)
 
         def normalise(q, j):
             if j == 0:
                 hn_sb[q] = work.tile([P, 2, WIDTH], F32, name="hn_sb", tag="hn_sb")
+            b = batch_of[q]
+            col = 2 * (q - first_of[b]) + j
             nc.gpsimd.tensor_scalar(
                 out=hn_sb[q][:, j, :].rearrange("r (t c i) -> r c t i", t=PACK, i=LINE),
                 in0=h_sb[q // 2][:, tile_cols(q, j)].rearrange("r (c i t) -> r c t i", t=PACK, i=LINE),
-                scalar1=rstd[q][:, j : j + 1],
+                scalar1=rstd[b][:, col : col + 1],
                 scalar2=0.0,
                 op0=ALU.mult,
                 op1=ALU.add,
@@ -208,7 +218,7 @@ def tile_hstu_pb_t_kernel(tc, x, h_attn, Wu, bu, g_norm, Wf, b_out, out):
         make_identity(nc, ident[:])
         ones = const.tile([P, P], BF16, name="ones")
         nc.vector.memset(ones[:], 1.0)
-        minus_half = const.tile([P, 2], F32, name="minus_half")
+        minus_half = const.tile([P, 2 * MAX_BATCH], F32, name="minus_half")
         nc.vector.memset(minus_half[:], -0.5)
         table = const.tile([P, 1], F32, name="table")
         nc.scalar.activation(out=table[:], in_=minus_half[:, 0:1], func=ACT.Silu)
@@ -221,8 +231,8 @@ def tile_hstu_pb_t_kernel(tc, x, h_attn, Wu, bu, g_norm, Wf, b_out, out):
         wf_scales = const.tile([P, WIDTH], U8, name="wf_scales", align_bytes=64)
         b_rows = const.tile([P, WIDTH], F32, name="b_rows")
 
-        square_sum(0, 0)
-        square_sum(0, 1)
+        square_sum(0)
+        square_sum(1)
         wu_banks, wf_banks = {}, {}
         for half in range(2):
             wu_banks[half] = psum.tile([P, 2, 2, P], F32, name="wu_ps", tag="z")
@@ -254,10 +264,10 @@ def tile_hstu_pb_t_kernel(tc, x, h_attn, Wu, bu, g_norm, Wf, b_out, out):
             transpose_h(0, j)
         for t in range(PACK):
             gain(0, t)
-        for q in (1, 2):
-            for j in range(2):
-                square_sum(q, j)
+        for tile in range(2, 6):
+            square_sum(tile)
         inverse_rms(1)
+        squared = 6
 
         def at(stage, q, *args):
             if 0 <= q < N_PAIRS:
@@ -271,19 +281,26 @@ def tile_hstu_pb_t_kernel(tc, x, h_attn, Wu, bu, g_norm, Wf, b_out, out):
                 at(multiply, p, j)
             for j in range(2):
                 at(project_out, p - 1, j)
+            at(transpose_x, p + 2)
             for t in range(PACK):
                 at(project_up, p + 1, t)
-            at(transpose_x, p + 2)
             for j in range(2):
                 at(normalise, p + 1, j)
             for j in range(2):
                 at(transpose_h, p + 1, j)
-            at(inverse_rms, p + 2)
-            at(square_sum, p + 3, 0)
+            if p + 2 in first_of:
+                inverse_rms(first_of.index(p + 2))
+            coming = [b for b in range(len(BATCHES)) if first_of[b] > p + 2]
+            if coming:
+                b = coming[0]
+                missing = 2 * (first_of[b] + BATCHES[b]) - squared
+                steps = first_of[b] - 2 - p
+                for tile in range(squared, squared + -(-missing // steps)):
+                    square_sum(tile)
+                squared += -(-missing // steps)
+            at(regroup_x, p + 2)
             for t in range(PACK):
                 at(silu, p + 1, t)
-            at(regroup_x, p + 2)
-            at(square_sum, p + 3, 1)
             for j in range(2):
                 at(add_bias, p - 1, j)
             at(quantise_uv, p)

@@ -22,7 +22,8 @@ N_PAIRS = TOKENS // PAIR
 LINE = 4
 AHEAD = 5
 MAX_BATCH = 4
-BATCHES = (1, 2, 2, 3) + (MAX_BATCH,) * 6
+GAIN_SCALAR = 1
+BATCHES = (1, 1, 1, 1, 1, 2, 2, 3) + (MAX_BATCH,) * 5
 RMS_EPS = 1.1920928955078125e-07
 FLOPS = 2 * 2 * TOKENS * WIDTH * WIDTH
 
@@ -134,13 +135,16 @@ def tile_hstu_pb_t_kernel(tc, x, h_attn, Wu, bu, g_norm, Wf, b_out, out):
 
         def silu(q, t):
             if t == 0:
-                u_sb[q] = work.tile([P, PACK, PAIR], F32, name="u_sb", tag="u_sb")
+                u_sb[q] = work.tile([P, PACK, PAIR], F32, name="u_sb", tag="u_sb", bufs=4)
             nc.scalar.activation(
                 out=u_sb[q][:, t, :], in_=z_ps[q, t // 2][:, t % 2, :], func=ACT.Silu, bias=bu_cols[:, t : t + 1], scale=1.0
             )
 
         def gain(q, t):
             nc.vector.tensor_scalar_mul(out=u_sb[q][:, t, :], in0=u_sb[q][:, t, :], scalar1=g_cols[:, t : t + 1])
+
+        def gain_scalar(q, t):
+            nc.scalar.activation(out=u_sb[q][:, t, :], in_=u_sb[q][:, t, :], func=ACT.Copy, scale=g_scale[:, t : t + 1])
 
         def transpose_h(q, j):
             ht_ps[q, j] = psum.tile([P, PACK, P], F32, name="ht", tag="ht", bufs=3)
@@ -220,6 +224,7 @@ def tile_hstu_pb_t_kernel(tc, x, h_attn, Wu, bu, g_norm, Wf, b_out, out):
         nc.vector.memset(ones[:], 1.0)
         minus_half = const.tile([P, 2 * MAX_BATCH], F32, name="minus_half")
         nc.vector.memset(minus_half[:], -0.5)
+        g_scale = const.tile([P, PACK], F32, name="g_scale")
         table = const.tile([P, 1], F32, name="table")
         nc.scalar.activation(out=table[:], in_=minus_half[:, 0:1], func=ACT.Silu)
 
@@ -246,7 +251,7 @@ def tile_hstu_pb_t_kernel(tc, x, h_attn, Wu, bu, g_norm, Wf, b_out, out):
         for q in range(2):
             transpose_x(q)
             regroup_x(q)
-        quantise_x(0)
+            quantise_x(q)
         for t in range(PACK):
             project_up(0, t)
         for t in range(PACK):
@@ -262,9 +267,20 @@ def tile_hstu_pb_t_kernel(tc, x, h_attn, Wu, bu, g_norm, Wf, b_out, out):
         nc.vector.tensor_copy(out=b_rows[:], in_=b_ps[:])
         for j in range(2):
             transpose_h(0, j)
+        nc.vector.tensor_copy(out=g_scale[:], in_=g_cols[:])
         for t in range(PACK):
             gain(0, t)
-        for tile in range(2, 6):
+        transpose_x(2)
+        regroup_x(2)
+        for tile in range(2, 4):
+            square_sum(tile)
+        for t in range(PACK):
+            project_up(1, t)
+        for t in range(PACK):
+            silu(1, t)
+        for t in range(GAIN_SCALAR):
+            gain_scalar(1, t)
+        for tile in range(4, 6):
             square_sum(tile)
         inverse_rms(1)
         squared = 6
@@ -276,14 +292,14 @@ def tile_hstu_pb_t_kernel(tc, x, h_attn, Wu, bu, g_norm, Wf, b_out, out):
         for p in range(N_PAIRS + 1):
             if p % 2 == 0 and p // 2 + AHEAD < N_LOADS:
                 load(p // 2 + AHEAD)
-            at(quantise_x, p + 1)
+            at(quantise_x, p + 2)
             for j in range(2):
                 at(multiply, p, j)
             for j in range(2):
                 at(project_out, p - 1, j)
-            at(transpose_x, p + 2)
+            at(transpose_x, p + 3)
             for t in range(PACK):
-                at(project_up, p + 1, t)
+                at(project_up, p + 2, t)
             for j in range(2):
                 at(normalise, p + 1, j)
             for j in range(2):
@@ -298,12 +314,14 @@ def tile_hstu_pb_t_kernel(tc, x, h_attn, Wu, bu, g_norm, Wf, b_out, out):
                 for tile in range(squared, squared + -(-missing // steps)):
                     square_sum(tile)
                 squared += -(-missing // steps)
-            at(regroup_x, p + 2)
+            at(regroup_x, p + 3)
             for t in range(PACK):
-                at(silu, p + 1, t)
+                at(silu, p + 2, t)
+            for t in range(GAIN_SCALAR):
+                at(gain_scalar, p + 2, t)
             for j in range(2):
                 at(add_bias, p - 1, j)
             at(quantise_uv, p)
-            for t in range(PACK):
+            for t in range(GAIN_SCALAR, PACK):
                 at(gain, p + 1, t)
             at(store, p - 1)

from contextlib import ExitStack

import concourse.mybir as mybir
from concourse.masks import make_identity

FP8X4 = mybir.dt.float8_e4m3fn_x4
BF16 = mybir.dt.bfloat16
F32 = mybir.dt.float32
U32 = mybir.dt.uint32
U8 = mybir.dt.uint8
ACT = mybir.ActivationFunctionType
ALU = mybir.AluOpType

P = 128
PACK = 4
WIDTH = P * PACK
TOKENS = 4 * 2048
LOAD_TILES = 4
N_LOADS = TOKENS // (LOAD_TILES * P)
PAIR = 2 * P
N_PAIRS = TOKENS // PAIR
LINE = 4
AHEAD = 5
MAX_BATCH = 4
GAIN_SCALAR = 1
BATCHES = (1, 1, 1, 1, 1, 2, 2, 3) + (MAX_BATCH,) * 5
RMS_EPS = 1.1920928955078125e-07
FLOPS = 2 * 2 * TOKENS * WIDTH * WIDTH


def tile_hstu_pb_t_kernel(tc, x, h_attn, Wu, bu, g_norm, Wf, b_out, out):
    nc = tc.nc
    x_loads = x.flatten_outer_dims().rearrange("(n p j) c -> n p (j c)", p=P, j=LOAD_TILES)
    h_loads = h_attn.flatten_outer_dims().rearrange("(n p j) c -> n p (j c)", p=P, j=LOAD_TILES)
    out_loads = out.flatten_outer_dims().rearrange("(n p j) c -> n p (j c)", p=P, j=LOAD_TILES)

    with ExitStack() as ctx:
        ctx.enter_context(tc.manual_schedule())
        const = ctx.enter_context(tc.tile_pool(name="const", bufs=1))
        loads = ctx.enter_context(tc.tile_pool(name="loads", bufs=7))
        work = ctx.enter_context(tc.tile_pool(name="work", bufs=3))
        psum = ctx.enter_context(tc.psum_pool(name="psum", bufs=2))

        x_sb, h_sb, hn_sb, sumsq, rstd = {}, {}, {}, {}, {}
        x_grouped, x_codes, x_scales = {}, {}, {}
        first_of = [sum(BATCHES[:b]) for b in range(len(BATCHES))]
        batch_of = [b for b in range(len(BATCHES)) for q in range(BATCHES[b])]
        u_sb, uv_grouped, uv_codes, uv_scales, o_sb = {}, {}, {}, {}, {}
        xt_ps, z_ps, ht_ps, o_ps = {}, {}, {}, {}

        def transpose_word_pair(bank, rows, first_col):
            words = rows[:].bitcast(F32)
            for l in range(2):
                for v in range(2):
                    col = first_col // 2 + l * (WIDTH // 2)
                    nc.tensor.transpose(bank[:, l, v, :], words[:, col + v : col + 2 * P : 2], ident[:])

        def regroup_word_pair(copy, bank, grouped, first):
            words = grouped[:].bitcast(F32)[:, first * 2 * P : (first + 2) * 2 * P]
            copy(
                out=words.rearrange("p (l w v) -> p l w v", l=2, v=2),
                in_=bank[:].rearrange("p l v w -> p l w v"),
            )

        def load(n):
            x_sb[n] = loads.tile([P, LOAD_TILES * WIDTH], BF16, name="x_sb", tag="x_sb")
            h_sb[n] = loads.tile([P, LOAD_TILES * WIDTH], BF16, name="h_sb", tag="h_sb")
            nc.sync.dma_start(out=x_sb[n][:], in_=x_loads[n])
            nc.sync.dma_start(out=h_sb[n][:], in_=h_loads[n])

        def tile_cols(q, j):
            first = (2 * (q % 2) + j) * WIDTH
            return slice(first, first + WIDTH)

        def square_sum(tile):
            q, j = divmod(tile, 2)
            b = batch_of[q]
            if b not in sumsq:
                sumsq[b] = work.tile([P, 2 * MAX_BATCH], F32, name="sumsq", tag="sumsq")
            col = tile - 2 * first_of[b]
            squares = work.tile([P, WIDTH], BF16, name="squares", tag="squares")
            nc.scalar.activation(
                out=squares[:], in_=h_sb[q // 2][:, tile_cols(q, j)], func=ACT.Square, accum_out=sumsq[b][:, col : col + 1]
            )

        def inverse_rms(b):
            n = 2 * BATCHES[b]
            mean = work.tile([P, 2 * MAX_BATCH], F32, name="mean", tag="mean")
            nc.gpsimd.tensor_scalar(
                out=mean[:, 0:n], in0=sumsq[b][:, 0:n], scalar1=1.0 / WIDTH, scalar2=RMS_EPS, op0=ALU.mult, op1=ALU.add
            )
            rstd[b] = work.tile([P, 2 * MAX_BATCH], F32, name="rstd", tag="rstd")
            nc.gpsimd.tensor_tensor(out=rstd[b][:, 0:n], in0=mean[:, 0:n], in1=minus_half[:, 0:n], op=ALU.pow)

        def normalise(q, j):
            if j == 0:
                hn_sb[q] = work.tile([P, 2, WIDTH], F32, name="hn_sb", tag="hn_sb")
            b = batch_of[q]
            col = 2 * (q - first_of[b]) + j
            nc.gpsimd.tensor_scalar(
                out=hn_sb[q][:, j, :].rearrange("r (t c i) -> r c t i", t=PACK, i=LINE),
                in0=h_sb[q // 2][:, tile_cols(q, j)].rearrange("r (c i t) -> r c t i", t=PACK, i=LINE),
                scalar1=rstd[b][:, col : col + 1],
                scalar2=0.0,
                op0=ALU.mult,
                op1=ALU.add,
            )

        def transpose_x(q):
            xt_ps[q] = psum.tile([P, 2, 2, P], F32, name="xt", tag="xt", bufs=1)
            transpose_word_pair(xt_ps[q], x_sb[q // 2], tile_cols(q, 0).start)

        def regroup_x(q):
            x_grouped[q] = work.tile([P, PAIR * PACK], BF16, name="x_grouped", tag="x_grouped", align_bytes=64)
            regroup_word_pair(nc.scalar.copy, xt_ps[q], x_grouped[q], 0)

        def quantise_x(q):
            x_codes[q] = work.tile([P, PAIR], U32, name="x_codes", tag="x_codes", align_bytes=64)
            x_scales[q] = work.tile([P, PAIR], U8, name="x_scales", tag="x_scales", align_bytes=64)
            nc.vector.quantize_mx(out=x_codes[q][:].bitcast(FP8X4), scales=x_scales[q][:], in_=x_grouped[q][:])

        def project_up(q, t):
            if t % 2 == 0:
                z_ps[q, t // 2] = psum.tile([P, 2, PAIR], F32, name="z", tag="z")
            cols = slice(t * P, (t + 1) * P)
            nc.tensor.matmul_mx(
                out=z_ps[q, t // 2][:, t % 2, :],
                lhsT=wu_codes[:, cols].bitcast(FP8X4),
                lhsT_scale=wu_scales[:, cols],
                rhs=x_codes[q][:].bitcast(FP8X4),
                rhs_scale=x_scales[q][:],
                start=True,
                stop=True,
            )

        def silu(q, t):
            if t == 0:
                u_sb[q] = work.tile([P, PACK, PAIR], F32, name="u_sb", tag="u_sb", bufs=4)
            nc.scalar.activation(
                out=u_sb[q][:, t, :], in_=z_ps[q, t // 2][:, t % 2, :], func=ACT.Silu, bias=bu_cols[:, t : t + 1], scale=1.0
            )

        def gain(q, t):
            nc.vector.tensor_scalar_mul(out=u_sb[q][:, t, :], in0=u_sb[q][:, t, :], scalar1=g_cols[:, t : t + 1])

        def gain_scalar(q, t):
            nc.scalar.activation(out=u_sb[q][:, t, :], in_=u_sb[q][:, t, :], func=ACT.Copy, scale=g_scale[:, t : t + 1])

        def transpose_h(q, j):
            ht_ps[q, j] = psum.tile([P, PACK, P], F32, name="ht", tag="ht", bufs=3)
            for t in range(PACK):
                nc.tensor.transpose(ht_ps[q, j][:, t, :], hn_sb[q][:, j, t * P : (t + 1) * P], ident[:])

        def multiply(q, j):
            if j == 0:
                uv_grouped[q] = work.tile([P, PAIR, PACK], BF16, name="uv_grouped", tag="uv_grouped", align_bytes=64)
            toks = slice(j * P, (j + 1) * P)
            nc.vector.tensor_tensor(
                out=uv_grouped[q][:, toks, :].rearrange("p (c i) t -> p c t i", i=LINE),
                in0=u_sb[q][:, :, toks].rearrange("p t (c i) -> p c t i", i=LINE),
                in1=ht_ps[q, j][:].rearrange("p t (c i) -> p c t i", i=LINE),
                op=ALU.mult,
            )

        def quantise_uv(q):
            uv_codes[q] = work.tile([P, PAIR], U32, name="uv_codes", tag="uv_codes", align_bytes=64)
            uv_scales[q] = work.tile([P, PAIR], U8, name="uv_scales", tag="uv_scales", align_bytes=64)
            nc.vector.quantize_mx(
                out=uv_codes[q][:].bitcast(FP8X4),
                scales=uv_scales[q][:],
                in_=uv_grouped[q][:].rearrange("p w t -> p (w t)"),
            )

        def project_out(q, j):
            o_ps[q, j] = psum.tile([P, WIDTH], F32, name="o", tag="o")
            toks = slice(j * P, (j + 1) * P)
            nc.tensor.matmul_mx(
                out=o_ps[q, j][:],
                lhsT=uv_codes[q][:, toks].bitcast(FP8X4),
                lhsT_scale=uv_scales[q][:, toks],
                rhs=wf_codes[:].bitcast(FP8X4),
                rhs_scale=wf_scales[:],
                start=True,
                stop=True,
            )

        def add_bias(q, j):
            if j == 0:
                o_sb[q] = work.tile([P, 2, WIDTH], F32, name="o_sb", tag="o_sb")
            nc.vector.tensor_tensor(out=o_sb[q][:, j, :], in0=o_ps[q, j][:], in1=b_rows[:], op=ALU.add)

        def store(q):
            first = 2 * (q % 2) * WIDTH
            nc.sync.dma_start(
                out=out_loads[q // 2][:, first : first + 2 * WIDTH], in_=o_sb[q][:].rearrange("p j c -> p (j c)")
            )

        x_sb[0] = loads.tile([P, LOAD_TILES * WIDTH], BF16, name="x_sb", tag="x_sb")
        h_sb[0] = loads.tile([P, LOAD_TILES * WIDTH], BF16, name="h_sb", tag="h_sb")
        wu_rows = const.tile([P, PACK * WIDTH], BF16, name="wu_rows")
        wf_rows = const.tile([P, PACK * WIDTH], BF16, name="wf_rows")
        bu_cols = const.tile([P, PACK], BF16, name="bu_cols")
        g_cols = const.tile([P, PACK], BF16, name="g_cols")
        b_row = const.tile([P, WIDTH], BF16, name="b_row")
        nc.vector.memset(b_row[:], 0.0)
        first_pair, second_pair = slice(0, 2 * WIDTH), slice(2 * WIDTH, 4 * WIDTH)
        nc.sync.dma_start(out=h_sb[0][:, first_pair], in_=h_loads[0][:, first_pair])
        nc.sync.dma_start(out=wu_rows[:], in_=Wu.rearrange("(p t) c -> p (t c)", t=PACK))
        nc.sync.dma_start(out=x_sb[0][:, first_pair], in_=x_loads[0][:, first_pair])
        nc.sync.dma_start(out=bu_cols[:], in_=bu.rearrange("(p t) -> p t", t=PACK))
        nc.sync.dma_start(out=g_cols[:], in_=g_norm.rearrange("(p t) -> p t", t=PACK))
        nc.sync.dma_start(out=b_row[0:1, :], in_=b_out.rearrange("(o c) -> o c", o=1))
        nc.sync.dma_start(out=x_sb[0][:, second_pair], in_=x_loads[0][:, second_pair])
        nc.sync.dma_start(
            out=wf_rows[:].rearrange("p (t c) -> p t c", t=PACK), in_=Wf.rearrange("(t p) c -> p t c", p=P)
        )
        nc.sync.dma_start(out=h_sb[0][:, second_pair], in_=h_loads[0][:, second_pair])
        for n in range(1, AHEAD):
            load(n)

        ident = const.tile([P, P], F32, name="ident")
        make_identity(nc, ident[:])
        ones = const.tile([P, P], BF16, name="ones")
        nc.vector.memset(ones[:], 1.0)
        minus_half = const.tile([P, 2 * MAX_BATCH], F32, name="minus_half")
        nc.vector.memset(minus_half[:], -0.5)
        g_scale = const.tile([P, PACK], F32, name="g_scale")
        table = const.tile([P, 1], F32, name="table")
        nc.scalar.activation(out=table[:], in_=minus_half[:, 0:1], func=ACT.Silu)

        wu_grouped = const.tile([P, WIDTH * PACK], BF16, name="wu_grouped", align_bytes=64)
        wu_codes = const.tile([P, WIDTH], U32, name="wu_codes", align_bytes=64)
        wu_scales = const.tile([P, WIDTH], U8, name="wu_scales", align_bytes=64)
        wf_grouped = const.tile([P, WIDTH * PACK], BF16, name="wf_grouped", align_bytes=64)
        wf_codes = const.tile([P, WIDTH], U32, name="wf_codes", align_bytes=64)
        wf_scales = const.tile([P, WIDTH], U8, name="wf_scales", align_bytes=64)
        b_rows = const.tile([P, WIDTH], F32, name="b_rows")

        square_sum(0)
        square_sum(1)
        wu_banks, wf_banks = {}, {}
        for half in range(2):
            wu_banks[half] = psum.tile([P, 2, 2, P], F32, name="wu_ps", tag="z")
            transpose_word_pair(wu_banks[half], wu_rows, 2 * half * WIDTH)
        regroup_word_pair(nc.vector.tensor_copy, wu_banks[0], wu_grouped, 0)
        regroup_word_pair(nc.scalar.copy, wu_banks[1], wu_grouped, 2)
        nc.vector.quantize_mx(out=wu_codes[:].bitcast(FP8X4), scales=wu_scales[:], in_=wu_grouped[:])
        inverse_rms(0)
        for j in range(2):
            normalise(0, j)
        for q in range(2):
            transpose_x(q)
            regroup_x(q)
            quantise_x(q)
        for t in range(PACK):
            project_up(0, t)
        for t in range(PACK):
            silu(0, t)

        for half in range(2):
            wf_banks[half] = psum.tile([P, 2, 2, P], F32, name="wf_ps", tag="o")
            transpose_word_pair(wf_banks[half], wf_rows, 2 * half * WIDTH)
            regroup_word_pair(nc.vector.tensor_copy, wf_banks[half], wf_grouped, 2 * half)
        b_ps = psum.tile([P, WIDTH], F32, name="b_ps", tag="ht", bufs=3)
        nc.tensor.matmul(out=b_ps[:], lhsT=ones[:], rhs=b_row[:], start=True, stop=True)
        nc.vector.quantize_mx(out=wf_codes[:].bitcast(FP8X4), scales=wf_scales[:], in_=wf_grouped[:])
        nc.vector.tensor_copy(out=b_rows[:], in_=b_ps[:])
        for j in range(2):
            transpose_h(0, j)
        nc.vector.tensor_copy(out=g_scale[:], in_=g_cols[:])
        for t in range(PACK):
            gain(0, t)
        transpose_x(2)
        regroup_x(2)
        for tile in range(2, 4):
            square_sum(tile)
        for t in range(PACK):
            project_up(1, t)
        for t in range(PACK):
            silu(1, t)
        for t in range(GAIN_SCALAR):
            gain_scalar(1, t)
        for tile in range(4, 6):
            square_sum(tile)
        inverse_rms(1)
        squared = 6

        def at(stage, q, *args):
            if 0 <= q < N_PAIRS:
                stage(q, *args)

        for p in range(N_PAIRS + 1):
            if p % 2 == 0 and p // 2 + AHEAD < N_LOADS:
                load(p // 2 + AHEAD)
            at(quantise_x, p + 2)
            for j in range(2):
                at(multiply, p, j)
            for j in range(2):
                at(project_out, p - 1, j)
            at(transpose_x, p + 3)
            for t in range(PACK):
                at(project_up, p + 2, t)
            for j in range(2):
                at(normalise, p + 1, j)
            for j in range(2):
                at(transpose_h, p + 1, j)
            if p + 2 in first_of:
                inverse_rms(first_of.index(p + 2))
            coming = [b for b in range(len(BATCHES)) if first_of[b] > p + 2]
            if coming:
                b = coming[0]
                missing = 2 * (first_of[b] + BATCHES[b]) - squared
                steps = first_of[b] - 2 - p
                for tile in range(squared, squared + -(-missing // steps)):
                    square_sum(tile)
                squared += -(-missing // steps)
            at(regroup_x, p + 3)
            for t in range(PACK):
                at(silu, p + 2, t)
            for t in range(GAIN_SCALAR):
                at(gain_scalar, p + 2, t)
            for j in range(2):
                at(add_bias, p - 1, j)
            at(quantise_uv, p)
            for t in range(GAIN_SCALAR, PACK):
                at(gain, p + 1, t)
            at(store, p - 1)
